import numpy as np
import ml_dtypes


def mxq(x, axis, fmt="e4m3"):
    dtype, down = {"e4m3": (ml_dtypes.float8_e4m3fn, 7), "e5m2": (ml_dtypes.float8_e5m2, 14)}[fmt]
    v = np.moveaxis(np.asarray(x, np.float32).astype(ml_dtypes.bfloat16).astype(np.float64), axis, -1)
    blocks = v.reshape(v.shape[:-1] + (-1, 32))
    amax = np.abs(blocks).max(-1, keepdims=True)
    byte = np.maximum(np.where(amax > 0, np.frexp(amax)[1] - 1 + 127, 0) - down, 1)
    scale = np.exp2(byte - 127.0)
    codes = (blocks / scale).astype(np.float32).astype(dtype).astype(np.float64)
    return np.moveaxis((codes * scale).reshape(v.shape), -1, axis)


WIDE = False


def mx_kscale(k):
    if not WIDE:
        return np.ones(k)
    levels = np.array([10, -10, 5, -5, 0])
    a = np.random.permutation(np.resize(levels, k // 512 * 4)).reshape(k // 512, 4)
    idx = np.arange(k)
    return np.exp2(a[idx // 512, idx % 128 // 32])


BF16 = ml_dtypes.bfloat16


def bf(x):
    return np.asarray(x, np.float32).astype(BF16)


def f64(x):
    return np.asarray(x).astype(np.float64)


B, S, HID, QK, H, C = 2, 1024, 1024, 1024, 8, 512
DK, DV = QK // H, HID // H
GFAST, GSLOW = 0.96875, 0.99609375


def setup_inputs():
    s = mx_kscale(S)
    lg = np.linspace(np.log(1.0 - GFAST), np.log(1.0 - GSLOW), H) + 0.3 * (np.random.random_sample(H) - 0.5)
    return {"q": bf(np.random.standard_normal((B, H, S, DK)) / DK ** 0.25),
            "k": bf(np.random.standard_normal((B, H, S, DK)) / DK ** 0.25 * s[:, None]),
            "v": bf(np.random.standard_normal((B, H, S, DV)) * 0.5 / s[:, None]),
            "gamma": bf(1.0 - np.exp(lg))}


def reference(q, k, v, gamma):
    q, k, g = f64(q), f64(k), f64(gamma)
    vq = mxq(f64(v), 2, "e4m3")
    idx = f64(np.arange(S))
    ret = np.zeros((B, H, S, DV))
    for i in range(S // C):
        r0, e = i * C, (i + 1) * C
        diff = idx[r0:e, None] - idx[None, :e]
        expn = np.maximum(diff, 0.0)
        dmask = np.where(diff >= 0, g[:, None, None] ** expn, 0.0)
        sc = (q[:, :, r0:e] @ k[:, :, :e].transpose(0, 1, 3, 2)) * dmask[None]
        ret[:, :, r0:e] = mxq(sc, 3, "e4m3") @ vq[:, :, :e]
    return ret

@@ -1,0 +1,162 @@
+from contextlib import ExitStack
+
+import concourse.mybir as mybir
+from concourse.masks import make_identity
+
+BF16 = mybir.dt.bfloat16
+F32 = mybir.dt.float32
+I32 = mybir.dt.int32
+U32 = mybir.dt.uint32
+U8 = mybir.dt.uint8
+FP8X4 = mybir.dt.float8_e4m3fn_x4
+ALU = mybir.AluOpType
+ACT = mybir.ActivationFunctionType
+
+B, H, S, D = 2, 8, 1024, 128
+P = 128
+PACK = 4
+TILES = S // P
+PASSES = TILES // PACK
+DIAG_BUFS = 4
+
+FLOPS = B * H * 2 * 2 * D * (512 * 512 + 512 * 1024)
+
+
+def tile_multiscaleretention_pa_kernel(tc, q, k, v, gamma, out):
+    nc = tc.nc
+    with ExitStack() as ctx:
+        const = ctx.enter_context(tc.tile_pool(name="const", bufs=1))
+        loads = ctx.enter_context(tc.tile_pool(name="loads", bufs=4))
+        operands = ctx.enter_context(tc.tile_pool(name="operands", bufs=2))
+        work = ctx.enter_context(tc.tile_pool(name="work", bufs=3))
+        transposed_psum = ctx.enter_context(tc.psum_pool(name="transposed_psum", bufs=2))
+        scores_psum = ctx.enter_context(tc.psum_pool(name="scores_psum", bufs=4))
+        out_psum = ctx.enter_context(tc.psum_pool(name="out_psum", bufs=2))
+
+        identity = const.tile([P, P], BF16)
+        make_identity(nc, identity[:])
+
+        gamma_bf = const.tile([P, H], BF16)
+        nc.sync.dma_start(out=gamma_bf[:], in_=gamma.partition_broadcast(P))
+        ln_gamma = const.tile([P, H], F32)
+        nc.scalar.activation(out=ln_gamma[:], in_=gamma_bf[:], func=ACT.Ln)
+
+        distance_int = const.tile([P, P, TILES], I32)
+        nc.gpsimd.iota(
+            distance_int[:],
+            pattern=[[1, P], [-P, TILES]],
+            base=P * (TILES - 1),
+            channel_multiplier=-1,
+        )
+        distance = const.tile([P, P, TILES], F32)
+        nc.vector.tensor_scalar_max(out=distance[:], in0=distance_int[:], scalar1=0.0)
+        causal = const.tile([P, P], F32)
+        nc.vector.tensor_single_scalar(
+            out=causal[:], in_=distance_int[:, :, TILES - 1], scalar=0.0, op=ALU.is_ge
+        )
+
+        diag_grouped = [
+            const.tile([P, PACK, P, PACK], BF16, name="diag_grouped%d" % i, align_bytes=64)
+            for i in range(DIAG_BUFS)
+        ]
+        for tile_ in diag_grouped:
+            nc.vector.memset(tile_[:], 0.0)
+
+        diag_groups_done = 0
+        for h in range(H):
+            decay = const.tile([P, P, TILES], F32, name="decay%d" % h)
+            nc.scalar.activation(
+                out=decay[:], in_=distance[:], func=ACT.Exp, scale=ln_gamma[:, h : h + 1]
+            )
+            nc.gpsimd.tensor_tensor(
+                out=decay[:, :, TILES - 1],
+                in0=decay[:, :, TILES - 1],
+                in1=causal[:],
+                op=ALU.mult,
+            )
+
+            for b in range(B):
+                k_sb = loads.tile([P, TILES, D], BF16, tag="k")
+                nc.sync.dma_start(out=k_sb[:], in_=k[b, h].rearrange("(j p) d -> p j d", p=P))
+                q_sb = loads.tile([P, TILES, D], BF16, tag="q")
+                nc.sync.dma_start(out=q_sb[:], in_=q[b, h].rearrange("(j p) d -> p j d", p=P))
+                v_sb = loads.tile([P, TILES, D], BF16, tag="v")
+                nc.sync.dma_start(out=v_sb[:], in_=v[b, h].rearrange("(j p) d -> p j d", p=P))
+
+                kT_ps = transposed_psum.tile([P, TILES, P], BF16, tag="transposed")
+                for j in range(TILES):
+                    nc.tensor.transpose(kT_ps[:, j, :], k_sb[:, j, :], identity[:])
+                kT = operands.tile([P, TILES, P], BF16, tag="kT")
+                nc.scalar.copy(out=kT[:], in_=kT_ps[:])
+                qT_ps = transposed_psum.tile([P, TILES, P], BF16, tag="transposed")
+                for j in range(TILES):
+                    nc.tensor.transpose(qT_ps[:, j, :], q_sb[:, j, :], identity[:])
+                qT = operands.tile([P, TILES, P], BF16, tag="qT")
+                nc.scalar.copy(out=qT[:], in_=qT_ps[:])
+
+                v_grouped = operands.tile([P, PASSES * D * PACK], BF16, tag="v_grouped", align_bytes=64)
+                nc.scalar.copy(
+                    out=v_grouped[:].rearrange("p (g d t) -> p g d t", g=PASSES, t=PACK),
+                    in_=v_sb[:].rearrange("p (g t) d -> p g d t", t=PACK),
+                )
+                v_codes = operands.tile([P, PASSES * D], U32, tag="v_codes", align_bytes=64)
+                v_scales = operands.tile([P, PASSES * D], U8, tag="v_scales", align_bytes=64)
+                nc.vector.quantize_mx(
+                    out=v_codes[:].bitcast(FP8X4), scales=v_scales[:], in_=v_grouped[:]
+                )
+
+                def masked_scores(first_query_tile, g, grouped):
+                    for u in range(PACK):
+                        query_tile = first_query_tile + u
+                        slots = min(PACK, query_tile - PACK * g + 1)
+                        bank = scores_psum.tile([P, PACK, P], F32, tag="scores")
+                        for t in range(slots):
+                            nc.tensor.matmul(
+                                bank[:, t, :],
+                                lhsT=kT[:, PACK * g + t, :],
+                                rhs=qT[:, query_tile, :],
+                                start=True,
+                                stop=True,
+                            )
+                        first = TILES - 1 - query_tile + PACK * g
+                        nc.vector.tensor_tensor(
+                            out=grouped[:, u, :, 0:slots],
+                            in0=bank[:, 0:slots, :].rearrange("p t c -> p c t"),
+                            in1=decay[:, :, first : first + slots],
+                            op=ALU.mult,
+                        )
+                    codes = work.tile([P, PACK * P], U32, tag="codes", align_bytes=64)
+                    scales = work.tile([P, PACK * P], U8, tag="scales", align_bytes=64)
+                    nc.vector.quantize_mx(
+                        out=codes[:].bitcast(FP8X4),
+                        scales=scales[:],
+                        in_=grouped[:].rearrange("p u c t -> p (u c t)"),
+                    )
+                    return codes, scales
+
+                def retention(chunk, quantised):
+                    acc = out_psum.tile([P, PACK, D], F32, tag="acc")
+                    for u in range(PACK):
+                        for g, (codes, scales) in enumerate(quantised):
+                            nc.tensor.matmul_mx(
+                                out=acc[:, u, :],
+                                lhsT=codes[:, u * P : (u + 1) * P].bitcast(FP8X4),
+                                lhsT_scale=scales[:, u * P : (u + 1) * P],
+                                rhs=v_codes[:, g * D : (g + 1) * D].bitcast(FP8X4),
+                                rhs_scale=v_scales[:, g * D : (g + 1) * D],
+                                start=(g == 0),
+                                stop=(g == len(quantised) - 1),
+                            )
+                    out_sb = work.tile([P, PACK, D], F32, tag="out_sb")
+                    nc.scalar.copy(out=out_sb[:], in_=acc[:])
+                    rows = out[b, h, chunk * PACK * P : (chunk + 1) * PACK * P, :]
+                    nc.scalar.dma_start(out=rows.rearrange("(j p) d -> p j d", p=P), in_=out_sb[:])
+
+                diag0 = masked_scores(0, 0, diag_grouped[diag_groups_done % DIAG_BUFS])
+                diag_groups_done += 1
+                retention(0, [diag0])
+                past_grouped = work.tile([P, PACK, P, PACK], BF16, tag="past_grouped", align_bytes=64)
+                past1 = masked_scores(PACK, 0, past_grouped)
+                diag1 = masked_scores(PACK, 1, diag_grouped[diag_groups_done % DIAG_BUFS])
+                diag_groups_done += 1
+                retention(1, [past1, diag1])

@@ -18,6 +18,8 @@ PACK = 4
 TILES = S // P
 PASSES = TILES // PACK
 DIAG_BUFS = 4
+GPSIMD_MAX_SLOTS = 2
+PAST_UNITS_ON_GPSIMD = 0
 
 FLOPS = B * H * 2 * 2 * D * (512 * 512 + 512 * 1024)
 
@@ -119,12 +121,27 @@ def tile_multiscaleretention_pa_kernel(tc, q, k, v, gamma, out):
                                 stop=True,
                             )
                         first = TILES - 1 - query_tile + PACK * g
-                        nc.vector.tensor_tensor(
-                            out=grouped[:, u, :, 0:slots],
-                            in0=bank[:, 0:slots, :].rearrange("p t c -> p c t"),
-                            in1=decay[:, :, first : first + slots],
-                            op=ALU.mult,
-                        )
+                        below_diagonal_chunk = g < query_tile // PACK
+                        if slots <= GPSIMD_MAX_SLOTS or (
+                            below_diagonal_chunk and u < PAST_UNITS_ON_GPSIMD
+                        ):
+                            staged = work.tile([P, P, slots], F32, tag="staged")
+                            nc.scalar.copy(
+                                out=staged[:], in_=bank[:, 0:slots, :].rearrange("p t c -> p c t")
+                            )
+                            nc.gpsimd.tensor_tensor(
+                                out=grouped[:, u, :, 0:slots],
+                                in0=staged[:],
+                                in1=decay[:, :, first : first + slots],
+                                op=ALU.mult,
+                            )
+                        else:
+                            nc.vector.tensor_tensor(
+                                out=grouped[:, u, :, 0:slots],
+                                in0=bank[:, 0:slots, :].rearrange("p t c -> p c t"),
+                                in1=decay[:, :, first : first + slots],
+                                op=ALU.mult,
+                            )
                     codes = work.tile([P, PACK * P], U32, tag="codes", align_bytes=64)
                     scales = work.tile([P, PACK * P], U8, tag="scales", align_bytes=64)
                     nc.vector.quantize_mx(

@@ -13,33 +13,193 @@ ALU = mybir.AluOpType
 ACT = mybir.ActivationFunctionType
 
 B, H, S, D = 2, 8, 1024, 128
+HEADS = B * H
 P = 128
 PACK = 4
 TILES = S // P
 PASSES = TILES // PACK
-DIAG_BUFS = 4
+SCORE_BANKS = 4
+
+DIAG0, PAST, DIAG1 = 0, 1, 2
+GROUPS = ((0, 0), (1, 0), (1, 1))
 GPSIMD_MAX_SLOTS = 2
-PAST_UNITS_ON_GPSIMD = 0
 
 FLOPS = B * H * 2 * 2 * D * (512 * 512 + 512 * 1024)
 
 
+def slots_of(group, u):
+    chunk, g = GROUPS[group]
+    return min(PACK, PACK * (chunk - g) + u + 1)
+
+
 def tile_multiscaleretention_pa_kernel(tc, q, k, v, gamma, out):
     nc = tc.nc
+    corner_units = [
+        (group, u)
+        for group in (DIAG1, DIAG0)
+        for u in range(PACK)
+        if slots_of(group, u) <= GPSIMD_MAX_SLOTS
+    ]
+    vector_units = [
+        (group, u)
+        for group in (DIAG0, PAST, DIAG1)
+        for u in range(PACK)
+        if slots_of(group, u) > GPSIMD_MAX_SLOTS
+    ]
+    head_units = corner_units + vector_units
+    sequence = [(i, group, u) for i in range(HEADS) for (group, u) in head_units]
+
     with ExitStack() as ctx:
         const = ctx.enter_context(tc.tile_pool(name="const", bufs=1))
-        loads = ctx.enter_context(tc.tile_pool(name="loads", bufs=4))
+        loads = ctx.enter_context(tc.tile_pool(name="loads", bufs=3))
         operands = ctx.enter_context(tc.tile_pool(name="operands", bufs=2))
-        work = ctx.enter_context(tc.tile_pool(name="work", bufs=3))
+        quantised = ctx.enter_context(tc.tile_pool(name="quantised", bufs=3))
+        staging = ctx.enter_context(tc.tile_pool(name="staging", bufs=4))
         transposed_psum = ctx.enter_context(tc.psum_pool(name="transposed_psum", bufs=2))
-        scores_psum = ctx.enter_context(tc.psum_pool(name="scores_psum", bufs=4))
+        scores_psum = ctx.enter_context(tc.psum_pool(name="scores_psum", bufs=SCORE_BANKS))
         out_psum = ctx.enter_context(tc.psum_pool(name="out_psum", bufs=2))
+        ctx.enter_context(tc.manual_schedule())
+
+        raw, transposed, kT, qT, v_mx, decay, banks, score_mx, accs = {}, {}, {}, {}, {}, {}, {}, {}, {}
+
+        def load(i):
+            h, b = divmod(i, B)
+            k_sb = loads.tile([P, TILES, D], BF16, tag="k")
+            nc.sync.dma_start(out=k_sb[:], in_=k[b, h].rearrange("(j p) d -> p j d", p=P))
+            q_sb = loads.tile([P, TILES, D], BF16, tag="q")
+            nc.sync.dma_start(out=q_sb[:], in_=q[b, h].rearrange("(j p) d -> p j d", p=P))
+            v_sb = loads.tile([P, TILES, D], BF16, tag="v")
+            nc.sync.dma_start(out=v_sb[:], in_=v[b, h].rearrange("(j p) d -> p j d", p=P))
+            raw[i] = (k_sb, q_sb, v_sb)
+
+        def decay_table(h):
+            table = const.tile([P, P, TILES], F32, name="decay%d" % h)
+            nc.scalar.activation(
+                out=table[:], in_=distance[:], func=ACT.Exp, scale=ln_gamma[:, h : h + 1]
+            )
+            nc.gpsimd.tensor_tensor(
+                out=table[:, :, TILES - 1], in0=table[:, :, TILES - 1], in1=causal[:], op=ALU.mult
+            )
+            decay[h] = table
+
+        def transpose(i):
+            k_sb, q_sb, v_sb = raw[i]
+            kT_ps = transposed_psum.tile([P, TILES, P], BF16, tag="transposed")
+            for j in range(TILES):
+                nc.tensor.transpose(kT_ps[:, j, :], k_sb[:, j, :], identity[:])
+            qT_ps = transposed_psum.tile([P, TILES, P], BF16, tag="transposed")
+            for j in range(TILES):
+                nc.tensor.transpose(qT_ps[:, j, :], q_sb[:, j, :], identity[:])
+            transposed[i] = (kT_ps, qT_ps)
+
+        def copy_transposed(i):
+            kT_ps, qT_ps = transposed[i]
+            kT_sb = operands.tile([P, TILES, P], BF16, tag="kT")
+            nc.scalar.copy(out=kT_sb[:], in_=kT_ps[:])
+            qT_sb = operands.tile([P, TILES, P], BF16, tag="qT")
+            nc.scalar.copy(out=qT_sb[:], in_=qT_ps[:])
+            kT[i], qT[i] = kT_sb, qT_sb
+
+        def regroup_v(i):
+            v_sb = raw[i][2]
+            v_grouped = operands.tile([P, PASSES * D * PACK], BF16, tag="v_grouped", align_bytes=64)
+            nc.scalar.copy(
+                out=v_grouped[:].rearrange("p (g d t) -> p g d t", g=PASSES, t=PACK),
+                in_=v_sb[:].rearrange("p (g t) d -> p g d t", t=PACK),
+            )
+            v_mx[i] = v_grouped
+
+        def quantise_v(i):
+            v_grouped = v_mx[i]
+            v_codes = operands.tile([P, PASSES * D], U32, tag="v_codes", align_bytes=64)
+            v_scales = operands.tile([P, PASSES * D], U8, tag="v_scales", align_bytes=64)
+            nc.vector.quantize_mx(out=v_codes[:].bitcast(FP8X4), scales=v_scales[:], in_=v_grouped[:])
+            v_mx[i] = (v_codes, v_scales)
+
+        def scores(i, group, u):
+            chunk, g = GROUPS[group]
+            bank = scores_psum.tile([P, PACK, P], F32, tag="scores")
+            for t in range(slots_of(group, u)):
+                nc.tensor.matmul(
+                    bank[:, t, :],
+                    lhsT=kT[i][:, PACK * g + t, :],
+                    rhs=qT[i][:, PACK * chunk + u, :],
+                    start=True,
+                    stop=True,
+                )
+            banks[(i, group, u)] = bank
+
+        def mask(i, group, u):
+            chunk, g = GROUPS[group]
+            slots = slots_of(group, u)
+            first = TILES - 1 - PACK * (chunk - g) - u
+            bank = banks[(i, group, u)]
+            scores_ct = bank[:, 0:slots, :].rearrange("p t c -> p c t")
+            decay_ct = decay[i // B][:, :, first : first + slots]
+            masked = grouped[group][:, u, :, 0:slots]
+            if slots <= GPSIMD_MAX_SLOTS:
+                staged = staging.tile([P, P, slots], F32, tag="staged")
+                nc.scalar.copy(out=staged[:], in_=scores_ct)
+                nc.gpsimd.tensor_tensor(out=masked, in0=staged[:], in1=decay_ct, op=ALU.mult)
+            else:
+                nc.vector.tensor_tensor(out=masked, in0=scores_ct, in1=decay_ct, op=ALU.mult)
+
+        def quantise(i, group):
+            codes = quantised.tile([P, PACK * P], U32, tag="codes", align_bytes=64)
+            scales = quantised.tile([P, PACK * P], U8, tag="scales", align_bytes=64)
+            nc.vector.quantize_mx(
+                out=codes[:].bitcast(FP8X4),
+                scales=scales[:],
+                in_=grouped[group][:].rearrange("p u c t -> p (u c t)"),
+            )
+            score_mx[(i, group)] = (codes, scales)
+
+        def retention(i, chunk):
+            v_codes, v_scales = v_mx[i]
+            groups = [group for group in (DIAG0, PAST, DIAG1) if GROUPS[group][0] == chunk]
+            acc = out_psum.tile([P, PACK, D], F32, tag="acc")
+            for u in range(PACK):
+                for group in groups:
+                    g = GROUPS[group][1]
+                    codes, scales = score_mx[(i, group)]
+                    nc.tensor.matmul_mx(
+                        out=acc[:, u, :],
+                        lhsT=codes[:, u * P : (u + 1) * P].bitcast(FP8X4),
+                        lhsT_scale=scales[:, u * P : (u + 1) * P],
+                        rhs=v_codes[:, g * D : (g + 1) * D].bitcast(FP8X4),
+                        rhs_scale=v_scales[:, g * D : (g + 1) * D],
+                        start=(group == groups[0]),
+                        stop=(group == groups[-1]),
+                    )
+            accs[(i, chunk)] = acc
+
+        def store(i, chunk):
+            h, b = divmod(i, B)
+            out_sb = staging.tile([P, PACK, D], F32, tag="out_sb")
+            nc.scalar.copy(out=out_sb[:], in_=accs[(i, chunk)][:])
+            rows = out[b, h, chunk * PACK * P : (chunk + 1) * PACK * P, :]
+            nc.sync.dma_start(out=rows.rearrange("(j p) d -> p j d", p=P), in_=out_sb[:])
+
+        def mask_and_refill(i, x):
+            mask(i, *head_units[x])
+            position = i * len(head_units) + x + SCORE_BANKS
+            if position < len(sequence):
+                scores(*sequence[position])
+
+        def finish(i):
+            for chunk in range(PASSES):
+                retention(i, chunk)
+            for chunk in range(PASSES):
+                store(i, chunk)
+
+        gamma_bf = const.tile([P, H], BF16)
+        nc.sync.dma_start(out=gamma_bf[:], in_=gamma.partition_broadcast(P))
+        load(0)
+        load(1)
 
         identity = const.tile([P, P], BF16)
         make_identity(nc, identity[:])
 
-        gamma_bf = const.tile([P, H], BF16)
-        nc.sync.dma_start(out=gamma_bf[:], in_=gamma.partition_broadcast(P))
         ln_gamma = const.tile([P, H], F32)
         nc.scalar.activation(out=ln_gamma[:], in_=gamma_bf[:], func=ACT.Ln)
 
@@ -50,6 +210,12 @@ def tile_multiscaleretention_pa_kernel(tc, q, k, v, gamma, out):
             base=P * (TILES - 1),
             channel_multiplier=-1,
         )
+        grouped = [
+            const.tile([P, PACK, P, PACK], BF16, name="grouped%d" % group, align_bytes=64)
+            for group in (DIAG0, PAST, DIAG1)
+        ]
+        nc.vector.memset(grouped[DIAG0][:], 0.0)
+        nc.vector.memset(grouped[DIAG1][:], 0.0)
         distance = const.tile([P, P, TILES], F32)
         nc.vector.tensor_scalar_max(out=distance[:], in0=distance_int[:], scalar1=0.0)
         causal = const.tile([P, P], F32)
@@ -57,123 +223,32 @@ def tile_multiscaleretention_pa_kernel(tc, q, k, v, gamma, out):
             out=causal[:], in_=distance_int[:, :, TILES - 1], scalar=0.0, op=ALU.is_ge
         )
 
-        diag_grouped = [
-            const.tile([P, PACK, P, PACK], BF16, name="diag_grouped%d" % i, align_bytes=64)
-            for i in range(DIAG_BUFS)
-        ]
-        for tile_ in diag_grouped:
-            nc.vector.memset(tile_[:], 0.0)
+        decay_table(0)
+        transpose(0)
+        copy_transposed(0)
+        regroup_v(0)
+        quantise_v(0)
+        for position in range(SCORE_BANKS):
+            scores(*sequence[position])
 
-        diag_groups_done = 0
-        for h in range(H):
-            decay = const.tile([P, P, TILES], F32, name="decay%d" % h)
-            nc.scalar.activation(
-                out=decay[:], in_=distance[:], func=ACT.Exp, scale=ln_gamma[:, h : h + 1]
-            )
-            nc.gpsimd.tensor_tensor(
-                out=decay[:, :, TILES - 1],
-                in0=decay[:, :, TILES - 1],
-                in1=causal[:],
-                op=ALU.mult,
-            )
-
-            for b in range(B):
-                k_sb = loads.tile([P, TILES, D], BF16, tag="k")
-                nc.sync.dma_start(out=k_sb[:], in_=k[b, h].rearrange("(j p) d -> p j d", p=P))
-                q_sb = loads.tile([P, TILES, D], BF16, tag="q")
-                nc.sync.dma_start(out=q_sb[:], in_=q[b, h].rearrange("(j p) d -> p j d", p=P))
-                v_sb = loads.tile([P, TILES, D], BF16, tag="v")
-                nc.sync.dma_start(out=v_sb[:], in_=v[b, h].rearrange("(j p) d -> p j d", p=P))
-
-                kT_ps = transposed_psum.tile([P, TILES, P], BF16, tag="transposed")
-                for j in range(TILES):
-                    nc.tensor.transpose(kT_ps[:, j, :], k_sb[:, j, :], identity[:])
-                kT = operands.tile([P, TILES, P], BF16, tag="kT")
-                nc.scalar.copy(out=kT[:], in_=kT_ps[:])
-                qT_ps = transposed_psum.tile([P, TILES, P], BF16, tag="transposed")
-                for j in range(TILES):
-                    nc.tensor.transpose(qT_ps[:, j, :], q_sb[:, j, :], identity[:])
-                qT = operands.tile([P, TILES, P], BF16, tag="qT")
-                nc.scalar.copy(out=qT[:], in_=qT_ps[:])
-
-                v_grouped = operands.tile([P, PASSES * D * PACK], BF16, tag="v_grouped", align_bytes=64)
-                nc.scalar.copy(
-                    out=v_grouped[:].rearrange("p (g d t) -> p g d t", g=PASSES, t=PACK),
-                    in_=v_sb[:].rearrange("p (g t) d -> p g d t", t=PACK),
-                )
-                v_codes = operands.tile([P, PASSES * D], U32, tag="v_codes", align_bytes=64)
-                v_scales = operands.tile([P, PASSES * D], U8, tag="v_scales", align_bytes=64)
-                nc.vector.quantize_mx(
-                    out=v_codes[:].bitcast(FP8X4), scales=v_scales[:], in_=v_grouped[:]
-                )
-
-                def masked_scores(first_query_tile, g, grouped):
-                    for u in range(PACK):
-                        query_tile = first_query_tile + u
-                        slots = min(PACK, query_tile - PACK * g + 1)
-                        bank = scores_psum.tile([P, PACK, P], F32, tag="scores")
-                        for t in range(slots):
-                            nc.tensor.matmul(
-                                bank[:, t, :],
-                                lhsT=kT[:, PACK * g + t, :],
-                                rhs=qT[:, query_tile, :],
-                                start=True,
-                                stop=True,
-                            )
-                        first = TILES - 1 - query_tile + PACK * g
-                        below_diagonal_chunk = g < query_tile // PACK
-                        if slots <= GPSIMD_MAX_SLOTS or (
-                            below_diagonal_chunk and u < PAST_UNITS_ON_GPSIMD
-                        ):
-                            staged = work.tile([P, P, slots], F32, tag="staged")
-                            nc.scalar.copy(
-                                out=staged[:], in_=bank[:, 0:slots, :].rearrange("p t c -> p c t")
-                            )
-                            nc.gpsimd.tensor_tensor(
-                                out=grouped[:, u, :, 0:slots],
-                                in0=staged[:],
-                                in1=decay[:, :, first : first + slots],
-                                op=ALU.mult,
-                            )
-                        else:
-                            nc.vector.tensor_tensor(
-                                out=grouped[:, u, :, 0:slots],
-                                in0=bank[:, 0:slots, :].rearrange("p t c -> p c t"),
-                                in1=decay[:, :, first : first + slots],
-                                op=ALU.mult,
-                            )
-                    codes = work.tile([P, PACK * P], U32, tag="codes", align_bytes=64)
-                    scales = work.tile([P, PACK * P], U8, tag="scales", align_bytes=64)
-                    nc.vector.quantize_mx(
-                        out=codes[:].bitcast(FP8X4),
-                        scales=scales[:],
-                        in_=grouped[:].rearrange("p u c t -> p (u c t)"),
-                    )
-                    return codes, scales
-
-                def retention(chunk, quantised):
-                    acc = out_psum.tile([P, PACK, D], F32, tag="acc")
-                    for u in range(PACK):
-                        for g, (codes, scales) in enumerate(quantised):
-                            nc.tensor.matmul_mx(
-                                out=acc[:, u, :],
-                                lhsT=codes[:, u * P : (u + 1) * P].bitcast(FP8X4),
-                                lhsT_scale=scales[:, u * P : (u + 1) * P],
-                                rhs=v_codes[:, g * D : (g + 1) * D].bitcast(FP8X4),
-                                rhs_scale=v_scales[:, g * D : (g + 1) * D],
-                                start=(g == 0),
-                                stop=(g == len(quantised) - 1),
-                            )
-                    out_sb = work.tile([P, PACK, D], F32, tag="out_sb")
-                    nc.scalar.copy(out=out_sb[:], in_=acc[:])
-                    rows = out[b, h, chunk * PACK * P : (chunk + 1) * PACK * P, :]
-                    nc.scalar.dma_start(out=rows.rearrange("(j p) d -> p j d", p=P), in_=out_sb[:])
-
-                diag0 = masked_scores(0, 0, diag_grouped[diag_groups_done % DIAG_BUFS])
-                diag_groups_done += 1
-                retention(0, [diag0])
-                past_grouped = work.tile([P, PACK, P, PACK], BF16, tag="past_grouped", align_bytes=64)
-                past1 = masked_scores(PACK, 0, past_grouped)
-                diag1 = masked_scores(PACK, 1, diag_grouped[diag_groups_done % DIAG_BUFS])
-                diag_groups_done += 1
-                retention(1, [past1, diag1])
+        for i in range(HEADS):
+            if i + 2 < HEADS:
+                load(i + 2)
+            for x in range(len(corner_units)):
+                mask_and_refill(i, x)
+            if i + 1 < HEADS:
+                regroup_v(i + 1)
+                if (i + 1) % B == 0:
+                    decay_table((i + 1) // B)
+                transpose(i + 1)
+                copy_transposed(i + 1)
+            if i > 0:
+                finish(i - 1)
+            for x in range(len(corner_units), len(head_units)):
+                mask_and_refill(i, x)
+            quantise(i, PAST)
+            quantise(i, DIAG0)
+            if i + 1 < HEADS:
+                quantise_v(i + 1)
+            quantise(i, DIAG1)
+        finish(HEADS - 1)

@@ -23,6 +23,7 @@ SCORE_BANKS = 4
 DIAG0, PAST, DIAG1 = 0, 1, 2
 GROUPS = ((0, 0), (1, 0), (1, 1))
 GPSIMD_MAX_SLOTS = 2
+PAST_UNITS_ON_GPSIMD = 1
 
 FLOPS = B * H * 2 * 2 * D * (512 * 512 + 512 * 1024)
 
@@ -32,19 +33,17 @@ def slots_of(group, u):
     return min(PACK, PACK * (chunk - g) + u + 1)
 
 
+def on_gpsimd(group, u):
+    return slots_of(group, u) <= GPSIMD_MAX_SLOTS or (group == PAST and u < PAST_UNITS_ON_GPSIMD)
+
+
 def tile_multiscaleretention_pa_kernel(tc, q, k, v, gamma, out):
     nc = tc.nc
     corner_units = [
-        (group, u)
-        for group in (DIAG1, DIAG0)
-        for u in range(PACK)
-        if slots_of(group, u) <= GPSIMD_MAX_SLOTS
+        (group, u) for group in (DIAG1, DIAG0, PAST) for u in range(PACK) if on_gpsimd(group, u)
     ]
     vector_units = [
-        (group, u)
-        for group in (DIAG0, PAST, DIAG1)
-        for u in range(PACK)
-        if slots_of(group, u) > GPSIMD_MAX_SLOTS
+        (group, u) for group in (DIAG0, PAST, DIAG1) for u in range(PACK) if not on_gpsimd(group, u)
     ]
     head_units = corner_units + vector_units
     sequence = [(i, group, u) for i in range(HEADS) for (group, u) in head_units]
@@ -54,7 +53,7 @@ def tile_multiscaleretention_pa_kernel(tc, q, k, v, gamma, out):
         loads = ctx.enter_context(tc.tile_pool(name="loads", bufs=3))
         operands = ctx.enter_context(tc.tile_pool(name="operands", bufs=2))
         quantised = ctx.enter_context(tc.tile_pool(name="quantised", bufs=3))
-        staging = ctx.enter_context(tc.tile_pool(name="staging", bufs=4))
+        staging = ctx.enter_context(tc.tile_pool(name="staging", bufs=len(corner_units)))
         transposed_psum = ctx.enter_context(tc.psum_pool(name="transposed_psum", bufs=2))
         scores_psum = ctx.enter_context(tc.psum_pool(name="scores_psum", bufs=SCORE_BANKS))
         out_psum = ctx.enter_context(tc.psum_pool(name="out_psum", bufs=2))
@@ -137,7 +136,7 @@ def tile_multiscaleretention_pa_kernel(tc, q, k, v, gamma, out):
             scores_ct = bank[:, 0:slots, :].rearrange("p t c -> p c t")
             decay_ct = decay[i // B][:, :, first : first + slots]
             masked = grouped[group][:, u, :, 0:slots]
-            if slots <= GPSIMD_MAX_SLOTS:
+            if on_gpsimd(group, u):
                 staged = staging.tile([P, P, slots], F32, tag="staged")
                 nc.scalar.copy(out=staged[:], in_=scores_ct)
                 nc.gpsimd.tensor_tensor(out=masked, in0=staged[:], in1=decay_ct, op=ALU.mult)
@@ -197,31 +196,33 @@ def tile_multiscaleretention_pa_kernel(tc, q, k, v, gamma, out):
         load(0)
         load(1)
 
-        identity = const.tile([P, P], BF16)
-        make_identity(nc, identity[:])
-
         ln_gamma = const.tile([P, H], F32)
         nc.scalar.activation(out=ln_gamma[:], in_=gamma_bf[:], func=ACT.Ln)
 
-        distance_int = const.tile([P, P, TILES], I32)
+        within_tile = const.tile([P, P], I32)
+        nc.gpsimd.iota(within_tile[:], pattern=[[1, P]], base=0, channel_multiplier=-1)
+        tiles_apart = const.tile([P, TILES], I32)
         nc.gpsimd.iota(
-            distance_int[:],
-            pattern=[[1, P], [-P, TILES]],
-            base=P * (TILES - 1),
-            channel_multiplier=-1,
+            tiles_apart[:], pattern=[[-P, TILES]], base=P * (TILES - 1), channel_multiplier=0
         )
+        identity = const.tile([P, P], BF16)
+        make_identity(nc, identity[:])
+        distance = const.tile([P, P, TILES], F32)
+        nc.vector.tensor_tensor(
+            out=distance[:],
+            in0=within_tile[:].unsqueeze(2).to_broadcast([P, P, TILES]),
+            in1=tiles_apart[:].unsqueeze(1).to_broadcast([P, P, TILES]),
+            op=ALU.add,
+        )
+        nc.vector.tensor_scalar_max(out=distance[:], in0=distance[:], scalar1=0.0)
+        causal = const.tile([P, P], F32)
+        nc.vector.tensor_single_scalar(out=causal[:], in_=within_tile[:], scalar=0.0, op=ALU.is_ge)
         grouped = [
             const.tile([P, PACK, P, PACK], BF16, name="grouped%d" % group, align_bytes=64)
             for group in (DIAG0, PAST, DIAG1)
         ]
         nc.vector.memset(grouped[DIAG0][:], 0.0)
         nc.vector.memset(grouped[DIAG1][:], 0.0)
-        distance = const.tile([P, P, TILES], F32)
-        nc.vector.tensor_scalar_max(out=distance[:], in0=distance_int[:], scalar1=0.0)
-        causal = const.tile([P, P], F32)
-        nc.vector.tensor_single_scalar(
-            out=causal[:], in_=distance_int[:, :, TILES - 1], scalar=0.0, op=ALU.is_ge
-        )
 
         decay_table(0)
         transpose(0)
@@ -246,9 +247,9 @@ def tile_multiscaleretention_pa_kernel(tc, q, k, v, gamma, out):
                 finish(i - 1)
             for x in range(len(corner_units), len(head_units)):
                 mask_and_refill(i, x)
-            quantise(i, PAST)
             quantise(i, DIAG0)
             if i + 1 < HEADS:
                 quantise_v(i + 1)
+            quantise(i, PAST)
             quantise(i, DIAG1)
         finish(HEADS - 1)

@@ -23,7 +23,6 @@ SCORE_BANKS = 4
 DIAG0, PAST, DIAG1 = 0, 1, 2
 GROUPS = ((0, 0), (1, 0), (1, 1))
 GPSIMD_MAX_SLOTS = 2
-PAST_UNITS_ON_GPSIMD = 1
 
 FLOPS = B * H * 2 * 2 * D * (512 * 512 + 512 * 1024)
 
@@ -34,13 +33,13 @@ def slots_of(group, u):
 
 
 def on_gpsimd(group, u):
-    return slots_of(group, u) <= GPSIMD_MAX_SLOTS or (group == PAST and u < PAST_UNITS_ON_GPSIMD)
+    return slots_of(group, u) <= GPSIMD_MAX_SLOTS
 
 
 def tile_multiscaleretention_pa_kernel(tc, q, k, v, gamma, out):
     nc = tc.nc
     corner_units = [
-        (group, u) for group in (DIAG1, DIAG0, PAST) for u in range(PACK) if on_gpsimd(group, u)
+        (group, u) for group in (DIAG1, DIAG0) for u in range(PACK) if on_gpsimd(group, u)
     ]
     vector_units = [
         (group, u) for group in (DIAG0, PAST, DIAG1) for u in range(PACK) if not on_gpsimd(group, u)
@@ -227,8 +226,6 @@ def tile_multiscaleretention_pa_kernel(tc, q, k, v, gamma, out):
         decay_table(0)
         transpose(0)
         copy_transposed(0)
-        regroup_v(0)
-        quantise_v(0)
         for position in range(SCORE_BANKS):
             scores(*sequence[position])
 
@@ -237,8 +234,8 @@ def tile_multiscaleretention_pa_kernel(tc, q, k, v, gamma, out):
                 load(i + 2)
             for x in range(len(corner_units)):
                 mask_and_refill(i, x)
+            regroup_v(i)
             if i + 1 < HEADS:
-                regroup_v(i + 1)
                 if (i + 1) % B == 0:
                     decay_table((i + 1) // B)
                 transpose(i + 1)
@@ -247,9 +244,8 @@ def tile_multiscaleretention_pa_kernel(tc, q, k, v, gamma, out):
                 finish(i - 1)
             for x in range(len(corner_units), len(head_units)):
                 mask_and_refill(i, x)
-            quantise(i, DIAG0)
-            if i + 1 < HEADS:
-                quantise_v(i + 1)
             quantise(i, PAST)
+            quantise(i, DIAG0)
+            quantise_v(i)
             quantise(i, DIAG1)
         finish(HEADS - 1)

from contextlib import ExitStack

import concourse.mybir as mybir
from concourse.masks import make_identity

BF16 = mybir.dt.bfloat16
F32 = mybir.dt.float32
I32 = mybir.dt.int32
U32 = mybir.dt.uint32
U8 = mybir.dt.uint8
FP8X4 = mybir.dt.float8_e4m3fn_x4
ALU = mybir.AluOpType
ACT = mybir.ActivationFunctionType

B, H, S, D = 2, 8, 1024, 128
HEADS = B * H
P = 128
PACK = 4
TILES = S // P
PASSES = TILES // PACK
SCORE_BANKS = 4

DIAG0, PAST, DIAG1 = 0, 1, 2
GROUPS = ((0, 0), (1, 0), (1, 1))
GPSIMD_MAX_SLOTS = 2

FLOPS = B * H * 2 * 2 * D * (512 * 512 + 512 * 1024)


def slots_of(group, u):
    chunk, g = GROUPS[group]
    return min(PACK, PACK * (chunk - g) + u + 1)


def on_gpsimd(group, u):
    return slots_of(group, u) <= GPSIMD_MAX_SLOTS


def tile_multiscaleretention_pa_kernel(tc, q, k, v, gamma, out):
    nc = tc.nc
    corner_units = [
        (group, u) for group in (DIAG1, DIAG0) for u in range(PACK) if on_gpsimd(group, u)
    ]
    vector_units = [
        (group, u) for group in (DIAG0, PAST, DIAG1) for u in range(PACK) if not on_gpsimd(group, u)
    ]
    head_units = corner_units + vector_units
    sequence = [(i, group, u) for i in range(HEADS) for (group, u) in head_units]

    with ExitStack() as ctx:
        const = ctx.enter_context(tc.tile_pool(name="const", bufs=1))
        loads = ctx.enter_context(tc.tile_pool(name="loads", bufs=3))
        operands = ctx.enter_context(tc.tile_pool(name="operands", bufs=2))
        quantised = ctx.enter_context(tc.tile_pool(name="quantised", bufs=3))
        staging = ctx.enter_context(tc.tile_pool(name="staging", bufs=len(corner_units)))
        transposed_psum = ctx.enter_context(tc.psum_pool(name="transposed_psum", bufs=2))
        scores_psum = ctx.enter_context(tc.psum_pool(name="scores_psum", bufs=SCORE_BANKS))
        out_psum = ctx.enter_context(tc.psum_pool(name="out_psum", bufs=2))
        ctx.enter_context(tc.manual_schedule())

        raw, transposed, kT, qT, v_mx, decay, banks, score_mx, accs = {}, {}, {}, {}, {}, {}, {}, {}, {}

        def load(i):
            h, b = divmod(i, B)
            k_sb = loads.tile([P, TILES, D], BF16, tag="k")
            nc.sync.dma_start(out=k_sb[:], in_=k[b, h].rearrange("(j p) d -> p j d", p=P))
            q_sb = loads.tile([P, TILES, D], BF16, tag="q")
            nc.sync.dma_start(out=q_sb[:], in_=q[b, h].rearrange("(j p) d -> p j d", p=P))
            v_sb = loads.tile([P, TILES, D], BF16, tag="v")
            nc.sync.dma_start(out=v_sb[:], in_=v[b, h].rearrange("(j p) d -> p j d", p=P))
            raw[i] = (k_sb, q_sb, v_sb)

        def decay_table(h):
            table = const.tile([P, P, TILES], F32, name="decay%d" % h)
            nc.scalar.activation(
                out=table[:], in_=distance[:], func=ACT.Exp, scale=ln_gamma[:, h : h + 1]
            )
            nc.gpsimd.tensor_tensor(
                out=table[:, :, TILES - 1], in0=table[:, :, TILES - 1], in1=causal[:], op=ALU.mult
            )
            decay[h] = table

        def transpose(i):
            k_sb, q_sb, v_sb = raw[i]
            kT_ps = transposed_psum.tile([P, TILES, P], BF16, tag="transposed")
            for j in range(TILES):
                nc.tensor.transpose(kT_ps[:, j, :], k_sb[:, j, :], identity[:])
            qT_ps = transposed_psum.tile([P, TILES, P], BF16, tag="transposed")
            for j in range(TILES):
                nc.tensor.transpose(qT_ps[:, j, :], q_sb[:, j, :], identity[:])
            transposed[i] = (kT_ps, qT_ps)

        def copy_transposed(i):
            kT_ps, qT_ps = transposed[i]
            kT_sb = operands.tile([P, TILES, P], BF16, tag="kT")
            nc.scalar.copy(out=kT_sb[:], in_=kT_ps[:])
            qT_sb = operands.tile([P, TILES, P], BF16, tag="qT")
            nc.scalar.copy(out=qT_sb[:], in_=qT_ps[:])
            kT[i], qT[i] = kT_sb, qT_sb

        def regroup_v(i):
            v_sb = raw[i][2]
            v_grouped = operands.tile([P, PASSES * D * PACK], BF16, tag="v_grouped", align_bytes=64)
            nc.scalar.copy(
                out=v_grouped[:].rearrange("p (g d t) -> p g d t", g=PASSES, t=PACK),
                in_=v_sb[:].rearrange("p (g t) d -> p g d t", t=PACK),
            )
            v_mx[i] = v_grouped

        def quantise_v(i):
            v_grouped = v_mx[i]
            v_codes = operands.tile([P, PASSES * D], U32, tag="v_codes", align_bytes=64)
            v_scales = operands.tile([P, PASSES * D], U8, tag="v_scales", align_bytes=64)
            nc.vector.quantize_mx(out=v_codes[:].bitcast(FP8X4), scales=v_scales[:], in_=v_grouped[:])
            v_mx[i] = (v_codes, v_scales)

        def scores(i, group, u):
            chunk, g = GROUPS[group]
            bank = scores_psum.tile([P, PACK, P], F32, tag="scores")
            for t in range(slots_of(group, u)):
                nc.tensor.matmul(
                    bank[:, t, :],
                    lhsT=kT[i][:, PACK * g + t, :],
                    rhs=qT[i][:, PACK * chunk + u, :],
                    start=True,
                    stop=True,
                )
            banks[(i, group, u)] = bank

        def mask(i, group, u):
            chunk, g = GROUPS[group]
            slots = slots_of(group, u)
            first = TILES - 1 - PACK * (chunk - g) - u
            bank = banks[(i, group, u)]
            scores_ct = bank[:, 0:slots, :].rearrange("p t c -> p c t")
            decay_ct = decay[i // B][:, :, first : first + slots]
            masked = grouped[group][:, u, :, 0:slots]
            if on_gpsimd(group, u):
                staged = staging.tile([P, P, slots], F32, tag="staged")
                nc.scalar.copy(out=staged[:], in_=scores_ct)
                nc.gpsimd.tensor_tensor(out=masked, in0=staged[:], in1=decay_ct, op=ALU.mult)
            else:
                nc.vector.tensor_tensor(out=masked, in0=scores_ct, in1=decay_ct, op=ALU.mult)

        def quantise(i, group):
            codes = quantised.tile([P, PACK * P], U32, tag="codes", align_bytes=64)
            scales = quantised.tile([P, PACK * P], U8, tag="scales", align_bytes=64)
            nc.vector.quantize_mx(
                out=codes[:].bitcast(FP8X4),
                scales=scales[:],
                in_=grouped[group][:].rearrange("p u c t -> p (u c t)"),
            )
            score_mx[(i, group)] = (codes, scales)

        def retention(i, chunk):
            v_codes, v_scales = v_mx[i]
            groups = [group for group in (DIAG0, PAST, DIAG1) if GROUPS[group][0] == chunk]
            acc = out_psum.tile([P, PACK, D], F32, tag="acc")
            for u in range(PACK):
                for group in groups:
                    g = GROUPS[group][1]
                    codes, scales = score_mx[(i, group)]
                    nc.tensor.matmul_mx(
                        out=acc[:, u, :],
                        lhsT=codes[:, u * P : (u + 1) * P].bitcast(FP8X4),
                        lhsT_scale=scales[:, u * P : (u + 1) * P],
                        rhs=v_codes[:, g * D : (g + 1) * D].bitcast(FP8X4),
                        rhs_scale=v_scales[:, g * D : (g + 1) * D],
                        start=(group == groups[0]),
                        stop=(group == groups[-1]),
                    )
            accs[(i, chunk)] = acc

        def store(i, chunk):
            h, b = divmod(i, B)
            out_sb = staging.tile([P, PACK, D], F32, tag="out_sb")
            nc.scalar.copy(out=out_sb[:], in_=accs[(i, chunk)][:])
            rows = out[b, h, chunk * PACK * P : (chunk + 1) * PACK * P, :]
            nc.sync.dma_start(out=rows.rearrange("(j p) d -> p j d", p=P), in_=out_sb[:])

        def mask_and_refill(i, x):
            mask(i, *head_units[x])
            position = i * len(head_units) + x + SCORE_BANKS
            if position < len(sequence):
                scores(*sequence[position])

        def finish(i):
            for chunk in range(PASSES):
                retention(i, chunk)
            for chunk in range(PASSES):
                store(i, chunk)

        gamma_bf = const.tile([P, H], BF16)
        nc.sync.dma_start(out=gamma_bf[:], in_=gamma.partition_broadcast(P))
        load(0)
        load(1)

        ln_gamma = const.tile([P, H], F32)
        nc.scalar.activation(out=ln_gamma[:], in_=gamma_bf[:], func=ACT.Ln)

        within_tile = const.tile([P, P], I32)
        nc.gpsimd.iota(within_tile[:], pattern=[[1, P]], base=0, channel_multiplier=-1)
        tiles_apart = const.tile([P, TILES], I32)
        nc.gpsimd.iota(
            tiles_apart[:], pattern=[[-P, TILES]], base=P * (TILES - 1), channel_multiplier=0
        )
        identity = const.tile([P, P], BF16)
        make_identity(nc, identity[:])
        distance = const.tile([P, P, TILES], F32)
        nc.vector.tensor_tensor(
            out=distance[:],
            in0=within_tile[:].unsqueeze(2).to_broadcast([P, P, TILES]),
            in1=tiles_apart[:].unsqueeze(1).to_broadcast([P, P, TILES]),
            op=ALU.add,
        )
        nc.vector.tensor_scalar_max(out=distance[:], in0=distance[:], scalar1=0.0)
        causal = const.tile([P, P], F32)
        nc.vector.tensor_single_scalar(out=causal[:], in_=within_tile[:], scalar=0.0, op=ALU.is_ge)
        grouped = [
            const.tile([P, PACK, P, PACK], BF16, name="grouped%d" % group, align_bytes=64)
            for group in (DIAG0, PAST, DIAG1)
        ]
        nc.vector.memset(grouped[DIAG0][:], 0.0)
        nc.vector.memset(grouped[DIAG1][:], 0.0)

        decay_table(0)
        transpose(0)
        copy_transposed(0)
        for position in range(SCORE_BANKS):
            scores(*sequence[position])

        for i in range(HEADS):
            if i + 2 < HEADS:
                load(i + 2)
            for x in range(len(corner_units)):
                mask_and_refill(i, x)
            regroup_v(i)
            if i + 1 < HEADS:
                if (i + 1) % B == 0:
                    decay_table((i + 1) // B)
                transpose(i + 1)
                copy_transposed(i + 1)
            if i > 0:
                finish(i - 1)
            for x in range(len(corner_units), len(head_units)):
                mask_and_refill(i, x)
            quantise(i, PAST)
            quantise(i, DIAG0)
            quantise_v(i)
            quantise(i, DIAG1)
        finish(HEADS - 1)
